import numpy as np
import ml_dtypes

BF16 = ml_dtypes.bfloat16


def bf(x):
    return np.asarray(x, np.float32).astype(BF16)


def f32(x):
    return np.asarray(x, np.float32)


def f64(x):
    return np.asarray(x).astype(np.float64)


def striped(idx):
    return np.tile(idx.reshape(-1, 16).T, (8, 1))


D, D2, S, T, N, H = 128, 256, 1024, 8, 8192, 512
NEG_SLOPE = 0.2


def setup_inputs():
    idx = np.concatenate([np.random.permutation(S)[:H] for _ in range(N // H)])
    return {"x": bf(np.random.standard_normal((D, S))), "w2": bf(np.random.standard_normal((D, D)) / np.sqrt(D)), "gain2": f32(1.0 + 0.1 * np.random.standard_normal((D, 1))), "beta2": f32(0.1 * np.random.standard_normal((D, 1))), "w1": bf(np.random.standard_normal((D2, D)) / np.sqrt(D2)), "gain1": f32(1.0 + 0.1 * np.random.standard_normal((D, 1))), "beta1": f32(0.1 * np.random.standard_normal((D, 1))), "offs": striped(idx)}


def reference(x, w2, gain2, beta2, w1, gain1, beta1, offs):
    idx = offs[:16].T.reshape(-1)
    pre = f64(w2).T @ f64(x)[:, idx]
    h = np.maximum(pre * f64(gain2) + f64(beta2), 0.0).reshape(D, S, T)
    cat = np.concatenate([h.max(axis=2), h.mean(axis=2)], axis=0)
    v = (f64(w1).T @ cat) * f64(gain1) + f64(beta1)
    return np.where(v >= 0.0, v, NEG_SLOPE * v)

@@ -1,0 +1,76 @@
+import concourse.mybir as mybir
+
+BF16, F32, U16 = mybir.dt.bfloat16, mybir.dt.float32, mybir.dt.uint16
+ALU = mybir.AluOpType
+ACT = mybir.ActivationFunctionType
+
+D = 128
+POINTS = 1024
+NEIGHBOURS = 8
+LIST = POINTS * NEIGHBOURS
+PIECE = 512
+PIECE_POINTS = PIECE // NEIGHBOURS
+OUT_BLOCK = 512
+PSUM_BANKS = 8
+NEG_SLOPE = 0.2
+
+FLOPS = 2 * D * D * LIST + 2 * (2 * D) * D * POINTS
+
+
+def tile_featureextraction_kernel(tc, x, w2, gain2, beta2, w1, gain1, beta1, offs, out):
+    nc = tc.nc
+    with (
+        tc.tile_pool(name="held", bufs=1) as held,
+        tc.tile_pool(name="work", bufs=3) as work,
+        tc.psum_pool(name="banks", bufs=PSUM_BANKS) as banks,
+        nc.allow_low_precision(reason="the reductions run in float32; only their results are rounded to bfloat16"),
+    ):
+        offsets = held.tile([D, LIST // 16], U16, name="offsets")
+        nc.sync.dma_start(offsets[:], offs)
+        x_sb = held.tile([D, POINTS], BF16, name="x_sb")
+        nc.scalar.dma_start(x_sb[:], x)
+        w2_sb = held.tile([D, D], BF16, name="w2_sb")
+        nc.sync.dma_start(w2_sb[:], w2)
+        gain2_sb = held.tile([D, 1], F32, name="gain2_sb")
+        nc.scalar.dma_start(gain2_sb[:], gain2)
+        beta2_sb = held.tile([D, 1], F32, name="beta2_sb")
+        nc.scalar.dma_start(beta2_sb[:], beta2)
+        w1_mx = held.tile([D, D], BF16, name="w1_mx")
+        nc.sync.dma_start(w1_mx[:], w1[0:D, :])
+        w1_mn = held.tile([D, D], BF16, name="w1_mn")
+        nc.sync.dma_start(w1_mn[:], w1[D : 2 * D, :])
+        gain1_sb = held.tile([D, 1], F32, name="gain1_sb")
+        nc.sync.dma_start(gain1_sb[:], gain1)
+        beta1_sb = held.tile([D, 1], F32, name="beta1_sb")
+        nc.sync.dma_start(beta1_sb[:], beta1)
+
+        w1_sum = held.tile([D, D], BF16, name="w1_sum")
+        nc.vector.tensor_scalar_mul(w1_sum[:], w1_mn[:], 1.0 / NEIGHBOURS)
+
+        mx = held.tile([D, POINTS], BF16, name="mx")
+        sums = held.tile([D, POINTS], BF16, name="sums")
+
+        for r in range(LIST // PIECE):
+            pre = banks.tile([D, PIECE], F32, name="pre", tag="bank")
+            piece_offsets = offsets[:, r * (PIECE // 16) : (r + 1) * (PIECE // 16)]
+            nc.tensor.matmul(pre[:], w2_sb[:], x_sb[:].indirect(piece_offsets), start=True, stop=True)
+
+            h = work.tile([D, PIECE], F32, name="h")
+            nc.scalar.activation(h[:], pre[:], ACT.Relu, bias=beta2_sb[:], scale=gain2_sb[:])
+
+            by_point = h[:].rearrange("e (n t) -> e n t", t=NEIGHBOURS)
+            points = slice(r * PIECE_POINTS, (r + 1) * PIECE_POINTS)
+            nc.vector.tensor_reduce(mx[:, points], by_point, axis=mybir.AxisListType.X, op=ALU.max)
+            nc.vector.tensor_reduce(sums[:, points], by_point, axis=mybir.AxisListType.X, op=ALU.add)
+
+        for c in range(POINTS // OUT_BLOCK):
+            block = slice(c * OUT_BLOCK, (c + 1) * OUT_BLOCK)
+            acc = banks.tile([D, OUT_BLOCK], F32, name="acc", tag="bank")
+            nc.tensor.matmul(acc[:], w1_mx[:], mx[:, block], start=True, stop=False)
+            nc.tensor.matmul(acc[:], w1_sum[:], sums[:, block], start=False, stop=True)
+
+            v = work.tile([D, OUT_BLOCK], F32, name="v")
+            nc.scalar.activation(v[:], acc[:], ACT.Identity, bias=beta1_sb[:], scale=gain1_sb[:])
+            result = work.tile([D, OUT_BLOCK], F32, name="result")
+            nc.vector.scalar_tensor_tensor(result[:], v[:], NEG_SLOPE, v[:], op0=ALU.mult, op1=ALU.max)
+            nc.sync.dma_start(out[:, block], result[:])

@@ -9,7 +9,9 @@ POINTS = 1024
 NEIGHBOURS = 8
 LIST = POINTS * NEIGHBOURS
 PIECE = 512
-PIECE_POINTS = PIECE // NEIGHBOURS
+STEP_PIECES = 2
+STEP = STEP_PIECES * PIECE
+STEP_POINTS = STEP // NEIGHBOURS
 OUT_BLOCK = 512
 PSUM_BANKS = 8
 NEG_SLOPE = 0.2
@@ -22,6 +24,7 @@ def tile_featureextraction_kernel(tc, x, w2, gain2, beta2, w1, gain1, beta1, off
     with (
         tc.tile_pool(name="held", bufs=1) as held,
         tc.tile_pool(name="work", bufs=3) as work,
+        tc.tile_pool(name="tree", bufs=2) as tree,
         tc.psum_pool(name="banks", bufs=PSUM_BANKS) as banks,
         nc.allow_low_precision(reason="the reductions run in float32; only their results are rounded to bfloat16"),
     ):
@@ -50,18 +53,28 @@ def tile_featureextraction_kernel(tc, x, w2, gain2, beta2, w1, gain1, beta1, off
         mx = held.tile([D, POINTS], BF16, name="mx")
         sums = held.tile([D, POINTS], BF16, name="sums")
 
-        for r in range(LIST // PIECE):
-            pre = banks.tile([D, PIECE], F32, name="pre", tag="bank")
-            piece_offsets = offsets[:, r * (PIECE // 16) : (r + 1) * (PIECE // 16)]
-            nc.tensor.matmul(pre[:], w2_sb[:], x_sb[:].indirect(piece_offsets), start=True, stop=True)
-
-            h = work.tile([D, PIECE], F32, name="h")
-            nc.scalar.activation(h[:], pre[:], ACT.Relu, bias=beta2_sb[:], scale=gain2_sb[:])
+        for s in range(LIST // STEP):
+            h = work.tile([D, STEP], F32, name="h")
+            for k in range(STEP_PIECES):
+                r = s * STEP_PIECES + k
+                pre = banks.tile([D, PIECE], F32, name="pre", tag="bank")
+                piece_offsets = offsets[:, r * (PIECE // 16) : (r + 1) * (PIECE // 16)]
+                nc.tensor.matmul(pre[:], w2_sb[:], x_sb[:].indirect(piece_offsets), start=True, stop=True)
+                nc.scalar.activation(
+                    h[:, k * PIECE : (k + 1) * PIECE], pre[:], ACT.Relu, bias=beta2_sb[:], scale=gain2_sb[:]
+                )
 
             by_point = h[:].rearrange("e (n t) -> e n t", t=NEIGHBOURS)
-            points = slice(r * PIECE_POINTS, (r + 1) * PIECE_POINTS)
+            points = slice(s * STEP_POINTS, (s + 1) * STEP_POINTS)
             nc.vector.tensor_reduce(mx[:, points], by_point, axis=mybir.AxisListType.X, op=ALU.max)
-            nc.vector.tensor_reduce(sums[:, points], by_point, axis=mybir.AxisListType.X, op=ALU.add)
+            if s % 2 == 0:
+                fours = tree.tile([D, STEP_POINTS, 4], F32, name="fours")
+                nc.gpsimd.tensor_tensor(fours[:], by_point[:, :, 0:4], by_point[:, :, 4:8], op=ALU.add)
+                twos = tree.tile([D, STEP_POINTS, 2], F32, name="twos")
+                nc.gpsimd.tensor_tensor(twos[:], fours[:, :, 0:2], fours[:, :, 2:4], op=ALU.add)
+                nc.gpsimd.tensor_tensor(sums[:, points].unsqueeze(2), twos[:, :, 0:1], twos[:, :, 1:2], op=ALU.add)
+            else:
+                nc.vector.tensor_reduce(sums[:, points], by_point, axis=mybir.AxisListType.X, op=ALU.add)
 
         for c in range(POINTS // OUT_BLOCK):
             block = slice(c * OUT_BLOCK, (c + 1) * OUT_BLOCK)

@@ -9,10 +9,11 @@ POINTS = 1024
 NEIGHBOURS = 8
 LIST = POINTS * NEIGHBOURS
 PIECE = 512
+PIECE_POINTS = PIECE // NEIGHBOURS
 STEP_PIECES = 2
 STEP = STEP_PIECES * PIECE
 STEP_POINTS = STEP // NEIGHBOURS
-OUT_BLOCK = 512
+WARM_UP_MATMULS = 5
 PSUM_BANKS = 8
 NEG_SLOPE = 0.2
 
@@ -23,7 +24,7 @@ def tile_featureextraction_kernel(tc, x, w2, gain2, beta2, w1, gain1, beta1, off
     nc = tc.nc
     with (
         tc.tile_pool(name="held", bufs=1) as held,
-        tc.tile_pool(name="work", bufs=3) as work,
+        tc.tile_pool(name="h_ring", bufs=4) as h_ring,
         tc.tile_pool(name="tree", bufs=2) as tree,
         tc.psum_pool(name="banks", bufs=PSUM_BANKS) as banks,
         nc.allow_low_precision(reason="the reductions run in float32; only their results are rounded to bfloat16"),
@@ -47,43 +48,60 @@ def tile_featureextraction_kernel(tc, x, w2, gain2, beta2, w1, gain1, beta1, off
         beta1_sb = held.tile([D, 1], F32, name="beta1_sb")
         nc.sync.dma_start(beta1_sb[:], beta1)
 
+        zero = held.tile([D, 1], F32, name="zero")
+        nc.vector.memset(zero[:], 0.0)
+        unused = held.tile([D, 1], F32, name="unused")
+        nc.scalar.activation(unused[:], zero[:], ACT.Relu)
+
+        zeros = held.tile([D, PIECE], BF16, name="zeros")
+        nc.gpsimd.memset(zeros[:], 0.0)
+        idle_product = banks.tile([D, PIECE], F32, name="idle_product", tag="bank")
+        for i in range(WARM_UP_MATMULS):
+            nc.tensor.matmul(idle_product[:], zeros[:, 0:D], zeros[:], start=True, stop=True)
+
         w1_sum = held.tile([D, D], BF16, name="w1_sum")
         nc.vector.tensor_scalar_mul(w1_sum[:], w1_mn[:], 1.0 / NEIGHBOURS)
 
         mx = held.tile([D, POINTS], BF16, name="mx")
         sums = held.tile([D, POINTS], BF16, name="sums")
+        v = held.tile([D, POINTS], F32, name="v")
+        result = held.tile([D, POINTS], F32, name="result")
 
         for s in range(LIST // STEP):
-            h = work.tile([D, STEP], F32, name="h")
+            sums_on_gpsimd = s % 2 == 0
+            h = h_ring.tile([D, STEP], F32, name="h")
             for k in range(STEP_PIECES):
                 r = s * STEP_PIECES + k
                 pre = banks.tile([D, PIECE], F32, name="pre", tag="bank")
                 piece_offsets = offsets[:, r * (PIECE // 16) : (r + 1) * (PIECE // 16)]
                 nc.tensor.matmul(pre[:], w2_sb[:], x_sb[:].indirect(piece_offsets), start=True, stop=True)
-                nc.scalar.activation(
-                    h[:, k * PIECE : (k + 1) * PIECE], pre[:], ACT.Relu, bias=beta2_sb[:], scale=gain2_sb[:]
-                )
 
-            by_point = h[:].rearrange("e (n t) -> e n t", t=NEIGHBOURS)
-            points = slice(s * STEP_POINTS, (s + 1) * STEP_POINTS)
-            nc.vector.tensor_reduce(mx[:, points], by_point, axis=mybir.AxisListType.X, op=ALU.max)
-            if s % 2 == 0:
+                h_piece = h[:, k * PIECE : (k + 1) * PIECE]
+                nc.scalar.activation(h_piece, pre[:], ACT.Relu, bias=beta2_sb[:], scale=gain2_sb[:])
+
+                by_point = h_piece.rearrange("e (n t) -> e n t", t=NEIGHBOURS)
+                points = slice(r * PIECE_POINTS, (r + 1) * PIECE_POINTS)
+                nc.vector.tensor_reduce(mx[:, points], by_point, axis=mybir.AxisListType.X, op=ALU.max)
+                if not sums_on_gpsimd:
+                    nc.vector.tensor_reduce(sums[:, points], by_point, axis=mybir.AxisListType.X, op=ALU.add)
+
+            if sums_on_gpsimd:
+                by_point = h[:].rearrange("e (n t) -> e n t", t=NEIGHBOURS)
+                points = slice(s * STEP_POINTS, (s + 1) * STEP_POINTS)
                 fours = tree.tile([D, STEP_POINTS, 4], F32, name="fours")
                 nc.gpsimd.tensor_tensor(fours[:], by_point[:, :, 0:4], by_point[:, :, 4:8], op=ALU.add)
                 twos = tree.tile([D, STEP_POINTS, 2], F32, name="twos")
                 nc.gpsimd.tensor_tensor(twos[:], fours[:, :, 0:2], fours[:, :, 2:4], op=ALU.add)
                 nc.gpsimd.tensor_tensor(sums[:, points].unsqueeze(2), twos[:, :, 0:1], twos[:, :, 1:2], op=ALU.add)
-            else:
-                nc.vector.tensor_reduce(sums[:, points], by_point, axis=mybir.AxisListType.X, op=ALU.add)
 
-        for c in range(POINTS // OUT_BLOCK):
-            block = slice(c * OUT_BLOCK, (c + 1) * OUT_BLOCK)
-            acc = banks.tile([D, OUT_BLOCK], F32, name="acc", tag="bank")
-            nc.tensor.matmul(acc[:], w1_mx[:], mx[:, block], start=True, stop=False)
-            nc.tensor.matmul(acc[:], w1_sum[:], sums[:, block], start=False, stop=True)
+        for s in range(LIST // STEP):
+            points = slice(s * STEP_POINTS, (s + 1) * STEP_POINTS)
+            acc = banks.tile([D, STEP_POINTS], F32, name="acc", tag="bank")
+            nc.tensor.matmul(acc[:], w1_mx[:], mx[:, points], start=True, stop=False)
+            nc.tensor.matmul(acc[:], w1_sum[:], sums[:, points], start=False, stop=True)
 
-            v = work.tile([D, OUT_BLOCK], F32, name="v")
-            nc.scalar.activation(v[:], acc[:], ACT.Identity, bias=beta1_sb[:], scale=gain1_sb[:])
-            result = work.tile([D, OUT_BLOCK], F32, name="result")
-            nc.vector.scalar_tensor_tensor(result[:], v[:], NEG_SLOPE, v[:], op0=ALU.mult, op1=ALU.max)
-            nc.sync.dma_start(out[:, block], result[:])
+            nc.scalar.activation(v[:, points], acc[:], ACT.Identity, bias=beta1_sb[:], scale=gain1_sb[:])
+            nc.vector.scalar_tensor_tensor(
+                result[:, points], v[:, points], NEG_SLOPE, v[:, points], op0=ALU.mult, op1=ALU.max
+            )
+            nc.sync.dma_start(out[:, points], result[:, points])

@@ -13,7 +13,6 @@ PIECE_POINTS = PIECE // NEIGHBOURS
 STEP_PIECES = 2
 STEP = STEP_PIECES * PIECE
 STEP_POINTS = STEP // NEIGHBOURS
-WARM_UP_MATMULS = 5
 PSUM_BANKS = 8
 NEG_SLOPE = 0.2
 
@@ -52,12 +51,6 @@ def tile_featureextraction_kernel(tc, x, w2, gain2, beta2, w1, gain1, beta1, off
         nc.vector.memset(zero[:], 0.0)
         unused = held.tile([D, 1], F32, name="unused")
         nc.scalar.activation(unused[:], zero[:], ACT.Relu)
-
-        zeros = held.tile([D, PIECE], BF16, name="zeros")
-        nc.gpsimd.memset(zeros[:], 0.0)
-        idle_product = banks.tile([D, PIECE], F32, name="idle_product", tag="bank")
-        for i in range(WARM_UP_MATMULS):
-            nc.tensor.matmul(idle_product[:], zeros[:, 0:D], zeros[:], start=True, stop=True)
 
         w1_sum = held.tile([D, D], BF16, name="w1_sum")
         nc.vector.tensor_scalar_mul(w1_sum[:], w1_mn[:], 1.0 / NEIGHBOURS)

@@ -47,11 +47,6 @@ def tile_featureextraction_kernel(tc, x, w2, gain2, beta2, w1, gain1, beta1, off
         beta1_sb = held.tile([D, 1], F32, name="beta1_sb")
         nc.sync.dma_start(beta1_sb[:], beta1)
 
-        zero = held.tile([D, 1], F32, name="zero")
-        nc.vector.memset(zero[:], 0.0)
-        unused = held.tile([D, 1], F32, name="unused")
-        nc.scalar.activation(unused[:], zero[:], ACT.Relu)
-
         w1_sum = held.tile([D, D], BF16, name="w1_sum")
         nc.vector.tensor_scalar_mul(w1_sum[:], w1_mn[:], 1.0 / NEIGHBOURS)
 

@@ -24,7 +24,6 @@ def tile_featureextraction_kernel(tc, x, w2, gain2, beta2, w1, gain1, beta1, off
     with (
         tc.tile_pool(name="held", bufs=1) as held,
         tc.tile_pool(name="h_ring", bufs=4) as h_ring,
-        tc.tile_pool(name="tree", bufs=2) as tree,
         tc.psum_pool(name="banks", bufs=PSUM_BANKS) as banks,
         nc.allow_low_precision(reason="the reductions run in float32; only their results are rounded to bfloat16"),
     ):
@@ -56,7 +55,6 @@ def tile_featureextraction_kernel(tc, x, w2, gain2, beta2, w1, gain1, beta1, off
         result = held.tile([D, POINTS], F32, name="result")
 
         for s in range(LIST // STEP):
-            sums_on_gpsimd = s % 2 == 0
             h = h_ring.tile([D, STEP], F32, name="h")
             for k in range(STEP_PIECES):
                 r = s * STEP_PIECES + k
@@ -67,20 +65,21 @@ def tile_featureextraction_kernel(tc, x, w2, gain2, beta2, w1, gain1, beta1, off
                 h_piece = h[:, k * PIECE : (k + 1) * PIECE]
                 nc.scalar.activation(h_piece, pre[:], ACT.Relu, bias=beta2_sb[:], scale=gain2_sb[:])
 
-                by_point = h_piece.rearrange("e (n t) -> e n t", t=NEIGHBOURS)
                 points = slice(r * PIECE_POINTS, (r + 1) * PIECE_POINTS)
-                nc.vector.tensor_reduce(mx[:, points], by_point, axis=mybir.AxisListType.X, op=ALU.max)
-                if not sums_on_gpsimd:
-                    nc.vector.tensor_reduce(sums[:, points], by_point, axis=mybir.AxisListType.X, op=ALU.add)
+                nc.vector.tensor_reduce(
+                    mx[:, points],
+                    h_piece.rearrange("e (n t) -> e n t", t=NEIGHBOURS),
+                    axis=mybir.AxisListType.X,
+                    op=ALU.max,
+                )
 
-            if sums_on_gpsimd:
-                by_point = h[:].rearrange("e (n t) -> e n t", t=NEIGHBOURS)
-                points = slice(s * STEP_POINTS, (s + 1) * STEP_POINTS)
-                fours = tree.tile([D, STEP_POINTS, 4], F32, name="fours")
-                nc.gpsimd.tensor_tensor(fours[:], by_point[:, :, 0:4], by_point[:, :, 4:8], op=ALU.add)
-                twos = tree.tile([D, STEP_POINTS, 2], F32, name="twos")
-                nc.gpsimd.tensor_tensor(twos[:], fours[:, :, 0:2], fours[:, :, 2:4], op=ALU.add)
-                nc.gpsimd.tensor_tensor(sums[:, points].unsqueeze(2), twos[:, :, 0:1], twos[:, :, 1:2], op=ALU.add)
+            by_point = h[:].rearrange("e (n t) -> e n t", t=NEIGHBOURS)
+            points = slice(s * STEP_POINTS, (s + 1) * STEP_POINTS)
+            fours = h_ring.tile([D, STEP_POINTS, NEIGHBOURS // 2], F32, name="fours")
+            nc.gpsimd.tensor_tensor(
+                fours[:], by_point[:, :, 0 : NEIGHBOURS // 2], by_point[:, :, NEIGHBOURS // 2 : NEIGHBOURS], op=ALU.add
+            )
+            nc.vector.tensor_reduce(sums[:, points], fours[:], axis=mybir.AxisListType.X, op=ALU.add)
 
         for s in range(LIST // STEP):
             points = slice(s * STEP_POINTS, (s + 1) * STEP_POINTS)

@@ -10,9 +10,7 @@ NEIGHBOURS = 8
 LIST = POINTS * NEIGHBOURS
 PIECE = 512
 PIECE_POINTS = PIECE // NEIGHBOURS
-STEP_PIECES = 2
-STEP = STEP_PIECES * PIECE
-STEP_POINTS = STEP // NEIGHBOURS
+OUT_BLOCK = 128
 PSUM_BANKS = 8
 NEG_SLOPE = 0.2
 
@@ -23,7 +21,7 @@ def tile_featureextraction_kernel(tc, x, w2, gain2, beta2, w1, gain1, beta1, off
     nc = tc.nc
     with (
         tc.tile_pool(name="held", bufs=1) as held,
-        tc.tile_pool(name="h_ring", bufs=4) as h_ring,
+        tc.tile_pool(name="ring", bufs=6) as ring,
         tc.psum_pool(name="banks", bufs=PSUM_BANKS) as banks,
         nc.allow_low_precision(reason="the reductions run in float32; only their results are rounded to bfloat16"),
     ):
@@ -54,39 +52,29 @@ def tile_featureextraction_kernel(tc, x, w2, gain2, beta2, w1, gain1, beta1, off
         v = held.tile([D, POINTS], F32, name="v")
         result = held.tile([D, POINTS], F32, name="result")
 
-        for s in range(LIST // STEP):
-            h = h_ring.tile([D, STEP], F32, name="h")
-            for k in range(STEP_PIECES):
-                r = s * STEP_PIECES + k
-                pre = banks.tile([D, PIECE], F32, name="pre", tag="bank")
-                piece_offsets = offsets[:, r * (PIECE // 16) : (r + 1) * (PIECE // 16)]
-                nc.tensor.matmul(pre[:], w2_sb[:], x_sb[:].indirect(piece_offsets), start=True, stop=True)
+        for r in range(LIST // PIECE):
+            pre = banks.tile([D, PIECE], F32, name="pre", tag="bank")
+            piece_offsets = offsets[:, r * (PIECE // 16) : (r + 1) * (PIECE // 16)]
+            nc.tensor.matmul(pre[:], w2_sb[:], x_sb[:].indirect(piece_offsets), start=True, stop=True)
 
-                h_piece = h[:, k * PIECE : (k + 1) * PIECE]
-                nc.scalar.activation(h_piece, pre[:], ACT.Relu, bias=beta2_sb[:], scale=gain2_sb[:])
+            h = ring.tile([D, PIECE_POINTS, NEIGHBOURS], F32, name="h")
+            nc.scalar.activation(
+                h[:].rearrange("e n t -> e (n t)"), pre[:], ACT.Relu, bias=beta2_sb[:], scale=gain2_sb[:]
+            )
 
-                points = slice(r * PIECE_POINTS, (r + 1) * PIECE_POINTS)
-                nc.vector.tensor_reduce(
-                    mx[:, points],
-                    h_piece.rearrange("e (n t) -> e n t", t=NEIGHBOURS),
-                    axis=mybir.AxisListType.X,
-                    op=ALU.max,
-                )
-
-            by_point = h[:].rearrange("e (n t) -> e n t", t=NEIGHBOURS)
-            points = slice(s * STEP_POINTS, (s + 1) * STEP_POINTS)
-            fours = h_ring.tile([D, STEP_POINTS, NEIGHBOURS // 2], F32, name="fours")
+            points = slice(r * PIECE_POINTS, (r + 1) * PIECE_POINTS)
+            nc.vector.tensor_reduce(mx[:, points], h[:], axis=mybir.AxisListType.X, op=ALU.max)
+            fours = ring.tile([D, PIECE_POINTS, NEIGHBOURS // 2], F32, name="fours")
             nc.gpsimd.tensor_tensor(
-                fours[:], by_point[:, :, 0 : NEIGHBOURS // 2], by_point[:, :, NEIGHBOURS // 2 : NEIGHBOURS], op=ALU.add
+                fours[:], h[:, :, 0 : NEIGHBOURS // 2], h[:, :, NEIGHBOURS // 2 : NEIGHBOURS], op=ALU.add
             )
             nc.vector.tensor_reduce(sums[:, points], fours[:], axis=mybir.AxisListType.X, op=ALU.add)
 
-        for s in range(LIST // STEP):
-            points = slice(s * STEP_POINTS, (s + 1) * STEP_POINTS)
-            acc = banks.tile([D, STEP_POINTS], F32, name="acc", tag="bank")
+        for c in range(POINTS // OUT_BLOCK):
+            points = slice(c * OUT_BLOCK, (c + 1) * OUT_BLOCK)
+            acc = banks.tile([D, OUT_BLOCK], F32, name="acc", tag="bank")
             nc.tensor.matmul(acc[:], w1_mx[:], mx[:, points], start=True, stop=False)
             nc.tensor.matmul(acc[:], w1_sum[:], sums[:, points], start=False, stop=True)
-
             nc.scalar.activation(v[:, points], acc[:], ACT.Identity, bias=beta1_sb[:], scale=gain1_sb[:])
             nc.vector.scalar_tensor_tensor(
                 result[:, points], v[:, points], NEG_SLOPE, v[:, points], op0=ALU.mult, op1=ALU.max

@@ -10,6 +10,9 @@ NEIGHBOURS = 8
 LIST = POINTS * NEIGHBOURS
 PIECE = 512
 PIECE_POINTS = PIECE // NEIGHBOURS
+STEP_PIECES = 2
+STEP_POINTS = STEP_PIECES * PIECE_POINTS
+STEPS = POINTS // STEP_POINTS
 OUT_BLOCK = 128
 PSUM_BANKS = 8
 NEG_SLOPE = 0.2
@@ -21,7 +24,7 @@ def tile_featureextraction_kernel(tc, x, w2, gain2, beta2, w1, gain1, beta1, off
     nc = tc.nc
     with (
         tc.tile_pool(name="held", bufs=1) as held,
-        tc.tile_pool(name="ring", bufs=6) as ring,
+        tc.tile_pool(name="ring", bufs=4) as ring,
         tc.psum_pool(name="banks", bufs=PSUM_BANKS) as banks,
         nc.allow_low_precision(reason="the reductions run in float32; only their results are rounded to bfloat16"),
     ):
@@ -45,30 +48,37 @@ def tile_featureextraction_kernel(tc, x, w2, gain2, beta2, w1, gain1, beta1, off
         nc.sync.dma_start(beta1_sb[:], beta1)
 
         w1_sum = held.tile([D, D], BF16, name="w1_sum")
-        nc.vector.tensor_scalar_mul(w1_sum[:], w1_mn[:], 1.0 / NEIGHBOURS)
+        nc.gpsimd.tensor_scalar_mul(w1_sum[:], w1_mn[:], 1.0 / NEIGHBOURS)
 
         mx = held.tile([D, POINTS], BF16, name="mx")
         sums = held.tile([D, POINTS], BF16, name="sums")
         v = held.tile([D, POINTS], F32, name="v")
         result = held.tile([D, POINTS], F32, name="result")
 
-        for r in range(LIST // PIECE):
-            pre = banks.tile([D, PIECE], F32, name="pre", tag="bank")
-            piece_offsets = offsets[:, r * (PIECE // 16) : (r + 1) * (PIECE // 16)]
-            nc.tensor.matmul(pre[:], w2_sb[:], x_sb[:].indirect(piece_offsets), start=True, stop=True)
-
-            h = ring.tile([D, PIECE_POINTS, NEIGHBOURS], F32, name="h")
-            nc.scalar.activation(
-                h[:].rearrange("e n t -> e (n t)"), pre[:], ACT.Relu, bias=beta2_sb[:], scale=gain2_sb[:]
-            )
-
-            points = slice(r * PIECE_POINTS, (r + 1) * PIECE_POINTS)
-            nc.vector.tensor_reduce(mx[:, points], h[:], axis=mybir.AxisListType.X, op=ALU.max)
-            fours = ring.tile([D, PIECE_POINTS, NEIGHBOURS // 2], F32, name="fours")
-            nc.gpsimd.tensor_tensor(
-                fours[:], h[:, :, 0 : NEIGHBOURS // 2], h[:, :, NEIGHBOURS // 2 : NEIGHBOURS], op=ALU.add
-            )
-            nc.vector.tensor_reduce(sums[:, points], fours[:], axis=mybir.AxisListType.X, op=ALU.add)
+        fours_of = {}
+        for s in range(STEPS + 1):
+            if s < STEPS:
+                h = ring.tile([D, STEP_POINTS, NEIGHBOURS], F32, name="h")
+                for k in range(STEP_PIECES):
+                    r = s * STEP_PIECES + k
+                    pre = banks.tile([D, PIECE], F32, name="pre", tag="bank")
+                    piece_offsets = offsets[:, r * (PIECE // 16) : (r + 1) * (PIECE // 16)]
+                    nc.tensor.matmul(pre[:], w2_sb[:], x_sb[:].indirect(piece_offsets), start=True, stop=True)
+                    h_piece = h[:, k * PIECE_POINTS : (k + 1) * PIECE_POINTS, :]
+                    nc.scalar.activation(
+                        h_piece.rearrange("e n t -> e (n t)"), pre[:], ACT.Relu, bias=beta2_sb[:], scale=gain2_sb[:]
+                    )
+                    nc.vector.tensor_reduce(
+                        mx[:, r * PIECE_POINTS : (r + 1) * PIECE_POINTS], h_piece, axis=mybir.AxisListType.X, op=ALU.max
+                    )
+                fours = ring.tile([D, STEP_POINTS, NEIGHBOURS // 2], F32, name="fours")
+                nc.gpsimd.tensor_tensor(
+                    fours[:], h[:, :, 0 : NEIGHBOURS // 2], h[:, :, NEIGHBOURS // 2 : NEIGHBOURS], op=ALU.add
+                )
+                fours_of[s] = fours
+            if s > 0:
+                points = slice((s - 1) * STEP_POINTS, s * STEP_POINTS)
+                nc.vector.tensor_reduce(sums[:, points], fours_of[s - 1][:], axis=mybir.AxisListType.X, op=ALU.add)
 
         for c in range(POINTS // OUT_BLOCK):
             points = slice(c * OUT_BLOCK, (c + 1) * OUT_BLOCK)

@@ -35,20 +35,19 @@ def tile_featureextraction_kernel(tc, x, w2, gain2, beta2, w1, gain1, beta1, off
         w2_sb = held.tile([D, D], BF16, name="w2_sb")
         nc.sync.dma_start(w2_sb[:], w2)
         gain2_sb = held.tile([D, 1], F32, name="gain2_sb")
-        nc.scalar.dma_start(gain2_sb[:], gain2)
+        nc.sync.dma_start(gain2_sb[:], gain2)
         beta2_sb = held.tile([D, 1], F32, name="beta2_sb")
-        nc.scalar.dma_start(beta2_sb[:], beta2)
-        w1_mx = held.tile([D, D], BF16, name="w1_mx")
-        nc.sync.dma_start(w1_mx[:], w1[0:D, :])
-        w1_mn = held.tile([D, D], BF16, name="w1_mn")
-        nc.sync.dma_start(w1_mn[:], w1[D : 2 * D, :])
+        nc.sync.dma_start(beta2_sb[:], beta2)
+        w1_sb = held.tile([D, 2, D], BF16, name="w1_sb")
+        nc.scalar.dma_start(w1_sb[:], w1.rearrange("(half e) m -> e half m", half=2))
+        w1_mx = w1_sb[:, 0, :]
         gain1_sb = held.tile([D, 1], F32, name="gain1_sb")
-        nc.sync.dma_start(gain1_sb[:], gain1)
+        nc.scalar.dma_start(gain1_sb[:], gain1)
         beta1_sb = held.tile([D, 1], F32, name="beta1_sb")
-        nc.sync.dma_start(beta1_sb[:], beta1)
+        nc.scalar.dma_start(beta1_sb[:], beta1)
 
         w1_sum = held.tile([D, D], BF16, name="w1_sum")
-        nc.gpsimd.tensor_scalar_mul(w1_sum[:], w1_mn[:], 1.0 / NEIGHBOURS)
+        nc.gpsimd.tensor_scalar_mul(w1_sum[:], w1_sb[:, 1, :], 1.0 / NEIGHBOURS)
 
         mx = held.tile([D, POINTS], BF16, name="mx")
         sums = held.tile([D, POINTS], BF16, name="sums")
@@ -83,7 +82,7 @@ def tile_featureextraction_kernel(tc, x, w2, gain2, beta2, w1, gain1, beta1, off
         for c in range(POINTS // OUT_BLOCK):
             points = slice(c * OUT_BLOCK, (c + 1) * OUT_BLOCK)
             acc = banks.tile([D, OUT_BLOCK], F32, name="acc", tag="bank")
-            nc.tensor.matmul(acc[:], w1_mx[:], mx[:, points], start=True, stop=False)
+            nc.tensor.matmul(acc[:], w1_mx, mx[:, points], start=True, stop=False)
             nc.tensor.matmul(acc[:], w1_sum[:], sums[:, points], start=False, stop=True)
             nc.scalar.activation(v[:, points], acc[:], ACT.Identity, bias=beta1_sb[:], scale=gain1_sb[:])
             nc.vector.scalar_tensor_tensor(

@@ -1,4 +1,5 @@
 import concourse.mybir as mybir
+from concourse.masks import make_identity
 
 BF16, F32, U16 = mybir.dt.bfloat16, mybir.dt.float32, mybir.dt.uint16
 ALU = mybir.AluOpType
@@ -13,7 +14,7 @@ PIECE_POINTS = PIECE // NEIGHBOURS
 STEP_PIECES = 2
 STEP_POINTS = STEP_PIECES * PIECE_POINTS
 STEPS = POINTS // STEP_POINTS
-OUT_BLOCK = 128
+TENSOR_STEPS = (STEPS - 3, STEPS - 2)
 PSUM_BANKS = 8
 NEG_SLOPE = 0.2
 
@@ -49,15 +50,22 @@ def tile_featureextraction_kernel(tc, x, w2, gain2, beta2, w1, gain1, beta1, off
         w1_sum = held.tile([D, D], BF16, name="w1_sum")
         nc.gpsimd.tensor_scalar_mul(w1_sum[:], w1_sb[:, 1, :], 1.0 / NEIGHBOURS)
 
+        identity_f32 = held.tile([D, D], F32, name="identity_f32")
+        make_identity(nc, identity_f32[:])
+        identity_bf16 = held.tile([D, D], BF16, name="identity_bf16")
+        make_identity(nc, identity_bf16[:])
+
         mx = held.tile([D, POINTS], BF16, name="mx")
         sums = held.tile([D, POINTS], BF16, name="sums")
         v = held.tile([D, POINTS], F32, name="v")
         result = held.tile([D, POINTS], F32, name="result")
 
+        h_of = {}
         fours_of = {}
         for s in range(STEPS + 1):
             if s < STEPS:
                 h = ring.tile([D, STEP_POINTS, NEIGHBOURS], F32, name="h")
+                h_of[s] = h
                 for k in range(STEP_PIECES):
                     r = s * STEP_PIECES + k
                     pre = banks.tile([D, PIECE], F32, name="pre", tag="bank")
@@ -70,18 +78,37 @@ def tile_featureextraction_kernel(tc, x, w2, gain2, beta2, w1, gain1, beta1, off
                     nc.vector.tensor_reduce(
                         mx[:, r * PIECE_POINTS : (r + 1) * PIECE_POINTS], h_piece, axis=mybir.AxisListType.X, op=ALU.max
                     )
-                fours = ring.tile([D, STEP_POINTS, NEIGHBOURS // 2], F32, name="fours")
-                nc.gpsimd.tensor_tensor(
-                    fours[:], h[:, :, 0 : NEIGHBOURS // 2], h[:, :, NEIGHBOURS // 2 : NEIGHBOURS], op=ALU.add
-                )
-                fours_of[s] = fours
-            if s > 0:
+                if s not in TENSOR_STEPS:
+                    fours = ring.tile([D, STEP_POINTS, 4], F32, name="fours")
+                    nc.gpsimd.tensor_tensor(fours[:], h[:, :, 0:4], h[:, :, 4:8], op=ALU.add)
+                    fours_of[s] = fours
+            if s - 1 in fours_of:
                 points = slice((s - 1) * STEP_POINTS, s * STEP_POINTS)
                 nc.vector.tensor_reduce(sums[:, points], fours_of[s - 1][:], axis=mybir.AxisListType.X, op=ALU.add)
 
-        for c in range(POINTS // OUT_BLOCK):
-            points = slice(c * OUT_BLOCK, (c + 1) * OUT_BLOCK)
-            acc = banks.tile([D, OUT_BLOCK], F32, name="acc", tag="bank")
+        turned_of = {}
+        for s in TENSOR_STEPS:
+            turned_sums = banks.tile([STEP_POINTS, D], F32, name="turned_sums", tag="bank")
+            for t in range(NEIGHBOURS):
+                nc.tensor.matmul(
+                    turned_sums[:],
+                    h_of[s][:, :, t],
+                    identity_f32[:],
+                    is_transpose=True,
+                    start=(t == 0),
+                    stop=(t == NEIGHBOURS - 1),
+                )
+            turned = ring.tile([STEP_POINTS, D], BF16, name="turned")
+            nc.scalar.copy(turned[:], turned_sums[:])
+            turned_of[s] = turned
+        for s in TENSOR_STEPS:
+            back = banks.tile([D, STEP_POINTS], BF16, name="back", tag="bank")
+            nc.tensor.transpose(back[:], turned_of[s][:], identity_bf16[:])
+            nc.scalar.copy(sums[:, s * STEP_POINTS : (s + 1) * STEP_POINTS], back[:])
+
+        for s in range(STEPS):
+            points = slice(s * STEP_POINTS, (s + 1) * STEP_POINTS)
+            acc = banks.tile([D, STEP_POINTS], F32, name="acc", tag="bank")
             nc.tensor.matmul(acc[:], w1_mx, mx[:, points], start=True, stop=False)
             nc.tensor.matmul(acc[:], w1_sum[:], sums[:, points], start=False, stop=True)
             nc.scalar.activation(v[:, points], acc[:], ACT.Identity, bias=beta1_sb[:], scale=gain1_sb[:])

@@ -14,7 +14,7 @@ PIECE_POINTS = PIECE // NEIGHBOURS
 STEP_PIECES = 2
 STEP_POINTS = STEP_PIECES * PIECE_POINTS
 STEPS = POINTS // STEP_POINTS
-TENSOR_STEPS = (STEPS - 3, STEPS - 2)
+TENSOR_STEPS = (STEPS - 4, STEPS - 3, STEPS - 2)
 PSUM_BANKS = 8
 NEG_SLOPE = 0.2
 

@@ -15,6 +15,7 @@ STEP_PIECES = 2
 STEP_POINTS = STEP_PIECES * PIECE_POINTS
 STEPS = POINTS // STEP_POINTS
 TENSOR_STEPS = (STEPS - 4, STEPS - 3, STEPS - 2)
+GPSIMD_STEP = STEPS - 5
 PSUM_BANKS = 8
 NEG_SLOPE = 0.2
 
@@ -81,7 +82,17 @@ def tile_featureextraction_kernel(tc, x, w2, gain2, beta2, w1, gain1, beta1, off
                 if s not in TENSOR_STEPS:
                     fours = ring.tile([D, STEP_POINTS, 4], F32, name="fours")
                     nc.gpsimd.tensor_tensor(fours[:], h[:, :, 0:4], h[:, :, 4:8], op=ALU.add)
-                    fours_of[s] = fours
+                    if s == GPSIMD_STEP:
+                        twos = ring.tile([D, STEP_POINTS, 2], F32, name="twos")
+                        nc.gpsimd.tensor_tensor(twos[:], fours[:, :, 0:2], fours[:, :, 2:4], op=ALU.add)
+                        nc.gpsimd.tensor_tensor(
+                            sums[:, s * STEP_POINTS : (s + 1) * STEP_POINTS].unsqueeze(2),
+                            twos[:, :, 0:1],
+                            twos[:, :, 1:2],
+                            op=ALU.add,
+                        )
+                    else:
+                        fours_of[s] = fours
             if s - 1 in fours_of:
                 points = slice((s - 1) * STEP_POINTS, s * STEP_POINTS)
                 nc.vector.tensor_reduce(sums[:, points], fours_of[s - 1][:], axis=mybir.AxisListType.X, op=ALU.add)

@@ -16,6 +16,7 @@ STEP_POINTS = STEP_PIECES * PIECE_POINTS
 STEPS = POINTS // STEP_POINTS
 TENSOR_STEPS = (STEPS - 4, STEPS - 3, STEPS - 2)
 GPSIMD_STEP = STEPS - 5
+BLOCKS_BEFORE_TURNING_BACK = 2
 PSUM_BANKS = 8
 NEG_SLOPE = 0.2
 
@@ -112,12 +113,12 @@ def tile_featureextraction_kernel(tc, x, w2, gain2, beta2, w1, gain1, beta1, off
             turned = ring.tile([STEP_POINTS, D], BF16, name="turned")
             nc.scalar.copy(turned[:], turned_sums[:])
             turned_of[s] = turned
-        for s in TENSOR_STEPS:
-            back = banks.tile([D, STEP_POINTS], BF16, name="back", tag="bank")
-            nc.tensor.transpose(back[:], turned_of[s][:], identity_bf16[:])
-            nc.scalar.copy(sums[:, s * STEP_POINTS : (s + 1) * STEP_POINTS], back[:])
-
         for s in range(STEPS):
+            if s == BLOCKS_BEFORE_TURNING_BACK:
+                for turned_step in TENSOR_STEPS:
+                    back = banks.tile([D, STEP_POINTS], BF16, name="back", tag="bank")
+                    nc.tensor.transpose(back[:], turned_of[turned_step][:], identity_bf16[:])
+                    nc.scalar.copy(sums[:, turned_step * STEP_POINTS : (turned_step + 1) * STEP_POINTS], back[:])
             points = slice(s * STEP_POINTS, (s + 1) * STEP_POINTS)
             acc = banks.tile([D, STEP_POINTS], F32, name="acc", tag="bank")
             nc.tensor.matmul(acc[:], w1_mx, mx[:, points], start=True, stop=False)

@@ -16,6 +16,7 @@ STEP_POINTS = STEP_PIECES * PIECE_POINTS
 STEPS = POINTS // STEP_POINTS
 TENSOR_STEPS = (STEPS - 4, STEPS - 3, STEPS - 2)
 GPSIMD_STEP = STEPS - 5
+FIRST_BLOCK_STEPS = 2
 BLOCKS_BEFORE_TURNING_BACK = 2
 PSUM_BANKS = 8
 NEG_SLOPE = 0.2
@@ -51,6 +52,12 @@ def tile_featureextraction_kernel(tc, x, w2, gain2, beta2, w1, gain1, beta1, off
 
         w1_sum = held.tile([D, D], BF16, name="w1_sum")
         nc.gpsimd.tensor_scalar_mul(w1_sum[:], w1_sb[:, 1, :], 1.0 / NEIGHBOURS)
+
+        scaled = {}
+        for name, tile in (("gain1", gain1_sb), ("beta1", beta1_sb)):
+            for part in (NEG_SLOPE, 1.0 - NEG_SLOPE):
+                scaled[name, part] = held.tile([D, 1], F32, name=f"{name}_{'low' if part == NEG_SLOPE else 'rest'}")
+                nc.gpsimd.tensor_scalar_mul(scaled[name, part][:], tile[:], part)
 
         identity_f32 = held.tile([D, D], F32, name="identity_f32")
         make_identity(nc, identity_f32[:])
@@ -100,6 +107,18 @@ def tile_featureextraction_kernel(tc, x, w2, gain2, beta2, w1, gain1, beta1, off
 
         turned_of = {}
         for s in TENSOR_STEPS:
+            if s == TENSOR_STEPS[-1]:
+                points = slice(0, FIRST_BLOCK_STEPS * STEP_POINTS)
+                acc = banks.tile([D, FIRST_BLOCK_STEPS * STEP_POINTS], F32, name="acc_first", tag="bank")
+                nc.tensor.matmul(acc[:], w1_mx, mx[:, points], start=True, stop=False)
+                nc.tensor.matmul(acc[:], w1_sum[:], sums[:, points], start=False, stop=True)
+                rest = held.tile([D, FIRST_BLOCK_STEPS * STEP_POINTS], F32, name="rest")
+                for target, func, part in ((v[:, points], ACT.Identity, NEG_SLOPE), (rest[:], ACT.Relu, 1.0 - NEG_SLOPE)):
+                    nc.scalar.activation(
+                        target, acc[:], func, bias=scaled["beta1", part][:], scale=scaled["gain1", part][:]
+                    )
+                nc.gpsimd.tensor_tensor(result[:, points], v[:, points], rest[:], op=ALU.add)
+                nc.sync.dma_start(out[:, points], result[:, points])
             turned_sums = banks.tile([STEP_POINTS, D], F32, name="turned_sums", tag="bank")
             for t in range(NEIGHBOURS):
                 nc.tensor.matmul(
@@ -113,8 +132,8 @@ def tile_featureextraction_kernel(tc, x, w2, gain2, beta2, w1, gain1, beta1, off
             turned = ring.tile([STEP_POINTS, D], BF16, name="turned")
             nc.scalar.copy(turned[:], turned_sums[:])
             turned_of[s] = turned
-        for s in range(STEPS):
-            if s == BLOCKS_BEFORE_TURNING_BACK:
+        for s in range(FIRST_BLOCK_STEPS, STEPS):
+            if s == FIRST_BLOCK_STEPS + BLOCKS_BEFORE_TURNING_BACK:
                 for turned_step in TENSOR_STEPS:
                     back = banks.tile([D, STEP_POINTS], BF16, name="back", tag="bank")
                     nc.tensor.transpose(back[:], turned_of[turned_step][:], identity_bf16[:])

@@ -118,7 +118,9 @@ def tile_featureextraction_kernel(tc, x, w2, gain2, beta2, w1, gain1, beta1, off
                         target, acc[:], func, bias=scaled["beta1", part][:], scale=scaled["gain1", part][:]
                     )
                 nc.gpsimd.tensor_tensor(result[:, points], v[:, points], rest[:], op=ALU.add)
-                nc.sync.dma_start(out[:, points], result[:, points])
+                for first in range(FIRST_BLOCK_STEPS):
+                    points = slice(first * STEP_POINTS, (first + 1) * STEP_POINTS)
+                    nc.sync.dma_start(out[:, points], result[:, points])
             turned_sums = banks.tile([STEP_POINTS, D], F32, name="turned_sums", tag="bank")
             for t in range(NEIGHBOURS):
                 nc.tensor.matmul(

@@ -17,7 +17,6 @@ STEPS = POINTS // STEP_POINTS
 TENSOR_STEPS = (STEPS - 4, STEPS - 3, STEPS - 2)
 GPSIMD_STEP = STEPS - 5
 FIRST_BLOCK_STEPS = 2
-BLOCKS_BEFORE_TURNING_BACK = 2
 PSUM_BANKS = 8
 NEG_SLOPE = 0.2
 
@@ -106,21 +105,8 @@ def tile_featureextraction_kernel(tc, x, w2, gain2, beta2, w1, gain1, beta1, off
                 nc.vector.tensor_reduce(sums[:, points], fours_of[s - 1][:], axis=mybir.AxisListType.X, op=ALU.add)
 
         turned_of = {}
-        for s in TENSOR_STEPS:
-            if s == TENSOR_STEPS[-1]:
-                points = slice(0, FIRST_BLOCK_STEPS * STEP_POINTS)
-                acc = banks.tile([D, FIRST_BLOCK_STEPS * STEP_POINTS], F32, name="acc_first", tag="bank")
-                nc.tensor.matmul(acc[:], w1_mx, mx[:, points], start=True, stop=False)
-                nc.tensor.matmul(acc[:], w1_sum[:], sums[:, points], start=False, stop=True)
-                rest = held.tile([D, FIRST_BLOCK_STEPS * STEP_POINTS], F32, name="rest")
-                for target, func, part in ((v[:, points], ACT.Identity, NEG_SLOPE), (rest[:], ACT.Relu, 1.0 - NEG_SLOPE)):
-                    nc.scalar.activation(
-                        target, acc[:], func, bias=scaled["beta1", part][:], scale=scaled["gain1", part][:]
-                    )
-                nc.gpsimd.tensor_tensor(result[:, points], v[:, points], rest[:], op=ALU.add)
-                for first in range(FIRST_BLOCK_STEPS):
-                    points = slice(first * STEP_POINTS, (first + 1) * STEP_POINTS)
-                    nc.sync.dma_start(out[:, points], result[:, points])
+
+        def add_neighbours(s):
             turned_sums = banks.tile([STEP_POINTS, D], F32, name="turned_sums", tag="bank")
             for t in range(NEIGHBOURS):
                 nc.tensor.matmul(
@@ -134,12 +120,26 @@ def tile_featureextraction_kernel(tc, x, w2, gain2, beta2, w1, gain1, beta1, off
             turned = ring.tile([STEP_POINTS, D], BF16, name="turned")
             nc.scalar.copy(turned[:], turned_sums[:])
             turned_of[s] = turned
-        for s in range(FIRST_BLOCK_STEPS, STEPS):
-            if s == FIRST_BLOCK_STEPS + BLOCKS_BEFORE_TURNING_BACK:
-                for turned_step in TENSOR_STEPS:
-                    back = banks.tile([D, STEP_POINTS], BF16, name="back", tag="bank")
-                    nc.tensor.transpose(back[:], turned_of[turned_step][:], identity_bf16[:])
-                    nc.scalar.copy(sums[:, turned_step * STEP_POINTS : (turned_step + 1) * STEP_POINTS], back[:])
+
+        def turn_back(s):
+            back = banks.tile([D, STEP_POINTS], BF16, name="back", tag="bank")
+            nc.tensor.transpose(back[:], turned_of[s][:], identity_bf16[:])
+            nc.scalar.copy(sums[:, s * STEP_POINTS : (s + 1) * STEP_POINTS], back[:])
+
+        def first_block():
+            points = slice(0, FIRST_BLOCK_STEPS * STEP_POINTS)
+            acc = banks.tile([D, FIRST_BLOCK_STEPS * STEP_POINTS], F32, name="acc_first", tag="bank")
+            nc.tensor.matmul(acc[:], w1_mx, mx[:, points], start=True, stop=False)
+            nc.tensor.matmul(acc[:], w1_sum[:], sums[:, points], start=False, stop=True)
+            rest = held.tile([D, FIRST_BLOCK_STEPS * STEP_POINTS], F32, name="rest")
+            for target, func, part in ((v[:, points], ACT.Identity, NEG_SLOPE), (rest[:], ACT.Relu, 1.0 - NEG_SLOPE)):
+                nc.scalar.activation(target, acc[:], func, bias=scaled["beta1", part][:], scale=scaled["gain1", part][:])
+            nc.gpsimd.tensor_tensor(result[:, points], v[:, points], rest[:], op=ALU.add)
+            for s in range(FIRST_BLOCK_STEPS):
+                points = slice(s * STEP_POINTS, (s + 1) * STEP_POINTS)
+                nc.sync.dma_start(out[:, points], result[:, points])
+
+        def block(s):
             points = slice(s * STEP_POINTS, (s + 1) * STEP_POINTS)
             acc = banks.tile([D, STEP_POINTS], F32, name="acc", tag="bank")
             nc.tensor.matmul(acc[:], w1_mx, mx[:, points], start=True, stop=False)
@@ -149,3 +149,15 @@ def tile_featureextraction_kernel(tc, x, w2, gain2, beta2, w1, gain1, beta1, off
                 result[:, points], v[:, points], NEG_SLOPE, v[:, points], op0=ALU.mult, op1=ALU.max
             )
             nc.sync.dma_start(out[:, points], result[:, points])
+
+        early_blocks = list(range(FIRST_BLOCK_STEPS, TENSOR_STEPS[0]))
+        for s in TENSOR_STEPS:
+            add_neighbours(s)
+            if s == TENSOR_STEPS[0]:
+                first_block()
+            if early_blocks:
+                block(early_blocks.pop(0))
+        for s in TENSOR_STEPS:
+            turn_back(s)
+        for s in range(TENSOR_STEPS[0], STEPS):
+            block(s)

@@ -50,13 +50,12 @@ def tile_featureextraction_kernel(tc, x, w2, gain2, beta2, w1, gain1, beta1, off
         nc.scalar.dma_start(beta1_sb[:], beta1)
 
         w1_sum = held.tile([D, D], BF16, name="w1_sum")
-        nc.gpsimd.tensor_scalar_mul(w1_sum[:], w1_sb[:, 1, :], 1.0 / NEIGHBOURS)
+        nc.vector.tensor_scalar_mul(w1_sum[:], w1_sb[:, 1, :], 1.0 / NEIGHBOURS)
 
-        scaled = {}
-        for name, tile in (("gain1", gain1_sb), ("beta1", beta1_sb)):
-            for part in (NEG_SLOPE, 1.0 - NEG_SLOPE):
-                scaled[name, part] = held.tile([D, 1], F32, name=f"{name}_{'low' if part == NEG_SLOPE else 'rest'}")
-                nc.gpsimd.tensor_scalar_mul(scaled[name, part][:], tile[:], part)
+        gain1_rest = held.tile([D, 1], F32, name="gain1_rest")
+        nc.vector.tensor_scalar_mul(gain1_rest[:], gain1_sb[:], NEG_SLOPE - 1.0)
+        beta1_rest = held.tile([D, 1], F32, name="beta1_rest")
+        nc.vector.tensor_scalar_mul(beta1_rest[:], beta1_sb[:], NEG_SLOPE - 1.0)
 
         identity_f32 = held.tile([D, D], F32, name="identity_f32")
         make_identity(nc, identity_f32[:])
@@ -132,8 +131,8 @@ def tile_featureextraction_kernel(tc, x, w2, gain2, beta2, w1, gain1, beta1, off
             nc.tensor.matmul(acc[:], w1_mx, mx[:, points], start=True, stop=False)
             nc.tensor.matmul(acc[:], w1_sum[:], sums[:, points], start=False, stop=True)
             rest = held.tile([D, FIRST_BLOCK_STEPS * STEP_POINTS], F32, name="rest")
-            for target, func, part in ((v[:, points], ACT.Identity, NEG_SLOPE), (rest[:], ACT.Relu, 1.0 - NEG_SLOPE)):
-                nc.scalar.activation(target, acc[:], func, bias=scaled["beta1", part][:], scale=scaled["gain1", part][:])
+            nc.scalar.activation(v[:, points], acc[:], ACT.Identity, bias=beta1_sb[:], scale=gain1_sb[:])
+            nc.scalar.activation(rest[:], acc[:], ACT.Relu, bias=beta1_rest[:], scale=gain1_rest[:])
             nc.gpsimd.tensor_tensor(result[:, points], v[:, points], rest[:], op=ALU.add)
             for s in range(FIRST_BLOCK_STEPS):
                 points = slice(s * STEP_POINTS, (s + 1) * STEP_POINTS)

@@ -49,18 +49,23 @@ def tile_featureextraction_kernel(tc, x, w2, gain2, beta2, w1, gain1, beta1, off
         beta1_sb = held.tile([D, 1], F32, name="beta1_sb")
         nc.scalar.dma_start(beta1_sb[:], beta1)
 
-        w1_sum = held.tile([D, D], BF16, name="w1_sum")
-        nc.vector.tensor_scalar_mul(w1_sum[:], w1_sb[:, 1, :], 1.0 / NEIGHBOURS)
-
-        gain1_rest = held.tile([D, 1], F32, name="gain1_rest")
-        nc.vector.tensor_scalar_mul(gain1_rest[:], gain1_sb[:], NEG_SLOPE - 1.0)
-        beta1_rest = held.tile([D, 1], F32, name="beta1_rest")
-        nc.vector.tensor_scalar_mul(beta1_rest[:], beta1_sb[:], NEG_SLOPE - 1.0)
+        zero = held.tile([D, 1], F32, name="zero")
+        nc.vector.memset(zero[:], 0.0)
+        relu_of_zero = held.tile([D, 1], F32, name="relu_of_zero")
+        nc.scalar.activation(relu_of_zero[:], zero[:], ACT.Relu)
 
         identity_f32 = held.tile([D, D], F32, name="identity_f32")
         make_identity(nc, identity_f32[:])
         identity_bf16 = held.tile([D, D], BF16, name="identity_bf16")
         make_identity(nc, identity_bf16[:])
+
+        w1_sum = held.tile([D, D], BF16, name="w1_sum")
+        nc.gpsimd.tensor_scalar_mul(w1_sum[:], w1_sb[:, 1, :], 1.0 / NEIGHBOURS)
+
+        gain1_rest = held.tile([D, 1], F32, name="gain1_rest")
+        nc.gpsimd.tensor_scalar_mul(gain1_rest[:], gain1_sb[:], NEG_SLOPE - 1.0)
+        beta1_rest = held.tile([D, 1], F32, name="beta1_rest")
+        nc.gpsimd.tensor_scalar_mul(beta1_rest[:], beta1_sb[:], NEG_SLOPE - 1.0)
 
         mx = held.tile([D, POINTS], BF16, name="mx")
         sums = held.tile([D, POINTS], BF16, name="sums")

import concourse.mybir as mybir
from concourse.masks import make_identity

BF16, F32, U16 = mybir.dt.bfloat16, mybir.dt.float32, mybir.dt.uint16
ALU = mybir.AluOpType
ACT = mybir.ActivationFunctionType

D = 128
POINTS = 1024
NEIGHBOURS = 8
LIST = POINTS * NEIGHBOURS
PIECE = 512
PIECE_POINTS = PIECE // NEIGHBOURS
STEP_PIECES = 2
STEP_POINTS = STEP_PIECES * PIECE_POINTS
STEPS = POINTS // STEP_POINTS
TENSOR_STEPS = (STEPS - 4, STEPS - 3, STEPS - 2)
GPSIMD_STEP = STEPS - 5
FIRST_BLOCK_STEPS = 2
PSUM_BANKS = 8
NEG_SLOPE = 0.2

FLOPS = 2 * D * D * LIST + 2 * (2 * D) * D * POINTS


def tile_featureextraction_kernel(tc, x, w2, gain2, beta2, w1, gain1, beta1, offs, out):
    nc = tc.nc
    with (
        tc.tile_pool(name="held", bufs=1) as held,
        tc.tile_pool(name="ring", bufs=4) as ring,
        tc.psum_pool(name="banks", bufs=PSUM_BANKS) as banks,
        nc.allow_low_precision(reason="the reductions run in float32; only their results are rounded to bfloat16"),
    ):
        offsets = held.tile([D, LIST // 16], U16, name="offsets")
        nc.sync.dma_start(offsets[:], offs)
        x_sb = held.tile([D, POINTS], BF16, name="x_sb")
        nc.scalar.dma_start(x_sb[:], x)
        w2_sb = held.tile([D, D], BF16, name="w2_sb")
        nc.sync.dma_start(w2_sb[:], w2)
        gain2_sb = held.tile([D, 1], F32, name="gain2_sb")
        nc.sync.dma_start(gain2_sb[:], gain2)
        beta2_sb = held.tile([D, 1], F32, name="beta2_sb")
        nc.sync.dma_start(beta2_sb[:], beta2)
        w1_sb = held.tile([D, 2, D], BF16, name="w1_sb")
        nc.scalar.dma_start(w1_sb[:], w1.rearrange("(half e) m -> e half m", half=2))
        w1_mx = w1_sb[:, 0, :]
        gain1_sb = held.tile([D, 1], F32, name="gain1_sb")
        nc.scalar.dma_start(gain1_sb[:], gain1)
        beta1_sb = held.tile([D, 1], F32, name="beta1_sb")
        nc.scalar.dma_start(beta1_sb[:], beta1)

        zero = held.tile([D, 1], F32, name="zero")
        nc.vector.memset(zero[:], 0.0)
        relu_of_zero = held.tile([D, 1], F32, name="relu_of_zero")
        nc.scalar.activation(relu_of_zero[:], zero[:], ACT.Relu)

        identity_f32 = held.tile([D, D], F32, name="identity_f32")
        make_identity(nc, identity_f32[:])
        identity_bf16 = held.tile([D, D], BF16, name="identity_bf16")
        make_identity(nc, identity_bf16[:])

        w1_sum = held.tile([D, D], BF16, name="w1_sum")
        nc.gpsimd.tensor_scalar_mul(w1_sum[:], w1_sb[:, 1, :], 1.0 / NEIGHBOURS)

        gain1_rest = held.tile([D, 1], F32, name="gain1_rest")
        nc.gpsimd.tensor_scalar_mul(gain1_rest[:], gain1_sb[:], NEG_SLOPE - 1.0)
        beta1_rest = held.tile([D, 1], F32, name="beta1_rest")
        nc.gpsimd.tensor_scalar_mul(beta1_rest[:], beta1_sb[:], NEG_SLOPE - 1.0)

        mx = held.tile([D, POINTS], BF16, name="mx")
        sums = held.tile([D, POINTS], BF16, name="sums")
        v = held.tile([D, POINTS], F32, name="v")
        result = held.tile([D, POINTS], F32, name="result")

        h_of = {}
        fours_of = {}
        for s in range(STEPS + 1):
            if s < STEPS:
                h = ring.tile([D, STEP_POINTS, NEIGHBOURS], F32, name="h")
                h_of[s] = h
                for k in range(STEP_PIECES):
                    r = s * STEP_PIECES + k
                    pre = banks.tile([D, PIECE], F32, name="pre", tag="bank")
                    piece_offsets = offsets[:, r * (PIECE // 16) : (r + 1) * (PIECE // 16)]
                    nc.tensor.matmul(pre[:], w2_sb[:], x_sb[:].indirect(piece_offsets), start=True, stop=True)
                    h_piece = h[:, k * PIECE_POINTS : (k + 1) * PIECE_POINTS, :]
                    nc.scalar.activation(
                        h_piece.rearrange("e n t -> e (n t)"), pre[:], ACT.Relu, bias=beta2_sb[:], scale=gain2_sb[:]
                    )
                    nc.vector.tensor_reduce(
                        mx[:, r * PIECE_POINTS : (r + 1) * PIECE_POINTS], h_piece, axis=mybir.AxisListType.X, op=ALU.max
                    )
                if s not in TENSOR_STEPS:
                    fours = ring.tile([D, STEP_POINTS, 4], F32, name="fours")
                    nc.gpsimd.tensor_tensor(fours[:], h[:, :, 0:4], h[:, :, 4:8], op=ALU.add)
                    if s == GPSIMD_STEP:
                        twos = ring.tile([D, STEP_POINTS, 2], F32, name="twos")
                        nc.gpsimd.tensor_tensor(twos[:], fours[:, :, 0:2], fours[:, :, 2:4], op=ALU.add)
                        nc.gpsimd.tensor_tensor(
                            sums[:, s * STEP_POINTS : (s + 1) * STEP_POINTS].unsqueeze(2),
                            twos[:, :, 0:1],
                            twos[:, :, 1:2],
                            op=ALU.add,
                        )
                    else:
                        fours_of[s] = fours
            if s - 1 in fours_of:
                points = slice((s - 1) * STEP_POINTS, s * STEP_POINTS)
                nc.vector.tensor_reduce(sums[:, points], fours_of[s - 1][:], axis=mybir.AxisListType.X, op=ALU.add)

        turned_of = {}

        def add_neighbours(s):
            turned_sums = banks.tile([STEP_POINTS, D], F32, name="turned_sums", tag="bank")
            for t in range(NEIGHBOURS):
                nc.tensor.matmul(
                    turned_sums[:],
                    h_of[s][:, :, t],
                    identity_f32[:],
                    is_transpose=True,
                    start=(t == 0),
                    stop=(t == NEIGHBOURS - 1),
                )
            turned = ring.tile([STEP_POINTS, D], BF16, name="turned")
            nc.scalar.copy(turned[:], turned_sums[:])
            turned_of[s] = turned

        def turn_back(s):
            back = banks.tile([D, STEP_POINTS], BF16, name="back", tag="bank")
            nc.tensor.transpose(back[:], turned_of[s][:], identity_bf16[:])
            nc.scalar.copy(sums[:, s * STEP_POINTS : (s + 1) * STEP_POINTS], back[:])

        def first_block():
            points = slice(0, FIRST_BLOCK_STEPS * STEP_POINTS)
            acc = banks.tile([D, FIRST_BLOCK_STEPS * STEP_POINTS], F32, name="acc_first", tag="bank")
            nc.tensor.matmul(acc[:], w1_mx, mx[:, points], start=True, stop=False)
            nc.tensor.matmul(acc[:], w1_sum[:], sums[:, points], start=False, stop=True)
            rest = held.tile([D, FIRST_BLOCK_STEPS * STEP_POINTS], F32, name="rest")
            nc.scalar.activation(v[:, points], acc[:], ACT.Identity, bias=beta1_sb[:], scale=gain1_sb[:])
            nc.scalar.activation(rest[:], acc[:], ACT.Relu, bias=beta1_rest[:], scale=gain1_rest[:])
            nc.gpsimd.tensor_tensor(result[:, points], v[:, points], rest[:], op=ALU.add)
            for s in range(FIRST_BLOCK_STEPS):
                points = slice(s * STEP_POINTS, (s + 1) * STEP_POINTS)
                nc.sync.dma_start(out[:, points], result[:, points])

        def block(s):
            points = slice(s * STEP_POINTS, (s + 1) * STEP_POINTS)
            acc = banks.tile([D, STEP_POINTS], F32, name="acc", tag="bank")
            nc.tensor.matmul(acc[:], w1_mx, mx[:, points], start=True, stop=False)
            nc.tensor.matmul(acc[:], w1_sum[:], sums[:, points], start=False, stop=True)
            nc.scalar.activation(v[:, points], acc[:], ACT.Identity, bias=beta1_sb[:], scale=gain1_sb[:])
            nc.vector.scalar_tensor_tensor(
                result[:, points], v[:, points], NEG_SLOPE, v[:, points], op0=ALU.mult, op1=ALU.max
            )
            nc.sync.dma_start(out[:, points], result[:, points])

        early_blocks = list(range(FIRST_BLOCK_STEPS, TENSOR_STEPS[0]))
        for s in TENSOR_STEPS:
            add_neighbours(s)
            if s == TENSOR_STEPS[0]:
                first_block()
            if early_blocks:
                block(early_blocks.pop(0))
        for s in TENSOR_STEPS:
            turn_back(s)
        for s in range(TENSOR_STEPS[0], STEPS):
            block(s)
